import numpy as np
import ml_dtypes


def mxq(x, axis, fmt="e4m3"):
    dtype, down = {"e4m3": (ml_dtypes.float8_e4m3fn, 7), "e5m2": (ml_dtypes.float8_e5m2, 14)}[fmt]
    v = np.moveaxis(np.asarray(x, np.float32).astype(ml_dtypes.bfloat16).astype(np.float64), axis, -1)
    blocks = v.reshape(v.shape[:-1] + (-1, 32))
    amax = np.abs(blocks).max(-1, keepdims=True)
    byte = np.maximum(np.where(amax > 0, np.frexp(amax)[1] - 1 + 127, 0) - down, 1)
    scale = np.exp2(byte - 127.0)
    codes = (blocks / scale).astype(np.float32).astype(dtype).astype(np.float64)
    return np.moveaxis((codes * scale).reshape(v.shape), -1, axis)


WIDE = False


def mx_kscale(k):
    if not WIDE:
        return np.ones(k)
    levels = np.array([10, -10, 5, -5, 0])
    a = np.random.permutation(np.resize(levels, k // 512 * 4)).reshape(k // 512, 4)
    idx = np.arange(k)
    return np.exp2(a[idx // 512, idx % 128 // 32])


BF16 = ml_dtypes.bfloat16


def bf(x):
    return np.asarray(x, np.float32).astype(BF16)


def f64(x):
    return np.asarray(x).astype(np.float64)


H, D, L = 3, 512, 128
HD = H * D


def split_heads(x):
    return x.reshape(L, H, D).transpose(1, 2, 0)


def setup_inputs():
    s = mx_kscale(D)
    return {"tokens": bf(np.random.standard_normal((D, L)) * s[:, None]),
            "Wq": bf(np.random.standard_normal((HD, D)) / np.sqrt(D) / s),
            "bq": bf(np.random.standard_normal(HD) * 0.2),
            "Wk": bf(np.random.standard_normal((HD, D)) / np.sqrt(D) / s),
            "bk": bf(np.random.standard_normal(HD) * 0.2)}


def reference(tokens, Wq, bq, Wk, bk):
    tq = mxq(f64(tokens), 0, "e4m3")
    q = split_heads((mxq(f64(Wq), 1, "e4m3") @ tq) + f64(bq)[:, None])
    k = split_heads((mxq(f64(Wk), 1, "e4m3") @ tq) + f64(bk)[:, None])
    scores = (mxq(q.transpose(0, 2, 1), 2, "e4m3") @ mxq(k, 1, "e4m3")) / np.sqrt(D)
    e = np.exp(scores - scores.max(0, keepdims=True))
    return e / e.sum(0, keepdims=True)

@@ -1,0 +1,216 @@
+from contextlib import ExitStack
+import math
+
+import concourse.mybir as mybir
+from concourse.masks import make_identity
+
+BF16 = mybir.dt.bfloat16
+F32 = mybir.dt.float32
+U32 = mybir.dt.uint32
+U8 = mybir.dt.uint8
+FP8X4 = mybir.dt.float8_e4m3fn_x4
+ALU = mybir.AluOpType
+ACT = mybir.ActivationFunctionType
+
+P = 128
+PACK = 4
+HEADS = 3
+D = 512
+L = 128
+J = D // L
+ROWS_PER_POSITION = HEADS * J
+HALVES = 2
+BIAS_SLOT = 16
+
+FLOPS = 2 * (2 * HEADS * D) * D * L + 2 * HEADS * L * L * D
+
+
+def tile_selfattention_pa_s_kernel(tc, tokens, Wq, bq, Wk, bk, out):
+    nc = tc.nc
+    weights = (Wq, Wk)
+    biases = (bq, bk)
+    chunks = [(w, h) for h in range(HEADS) for w in range(2)]
+    n_chunks = len(chunks)
+
+    with ExitStack() as ctx:
+        keep = ctx.enter_context(tc.tile_pool(name="keep", bufs=1))
+        stage = ctx.enter_context(tc.tile_pool(name="stage", bufs=3))
+        psum_t = ctx.enter_context(tc.psum_pool(name="psum_t", bufs=4))
+        psum_acc = ctx.enter_context(tc.psum_pool(name="psum_acc", bufs=3))
+        psum_score = ctx.enter_context(tc.psum_pool(name="psum_score", bufs=1))
+        ctx.enter_context(tc.manual_schedule())
+
+        bias_in = keep.tile([P, 2, BIAS_SLOT], BF16)
+        for w in range(2):
+            nc.scalar.dma_start(
+                out=bias_in[:, w, 0:ROWS_PER_POSITION],
+                in_=biases[w].rearrange("(l r) -> l r", r=ROWS_PER_POSITION),
+            )
+        tok_raw = keep.tile([P, PACK, L], BF16)
+        nc.scalar.dma_start(
+            out=tok_raw[:].rearrange("p (u e) c -> p u (e c)", u=HALVES),
+            in_=tokens.rearrange("(u p e) c -> p u (e c)", u=HALVES, e=2),
+        )
+        w_raw = []
+        for i, (w, h) in enumerate(chunks):
+            raw = keep.tile([P, J * D], BF16, name="w_raw%d" % i)
+            nc.sync.dma_start(
+                out=raw[:],
+                in_=weights[w].rearrange("(l h j) k -> l h (j k)", h=HEADS, j=J)[:, h, :],
+            )
+            w_raw.append(raw)
+
+        ident = keep.tile([P, P], F32)
+        make_identity(nc, ident[:])
+        warm_in = keep.tile([P, 1], F32)
+        warm_out = keep.tile([P, 1], F32)
+        nc.vector.memset(warm_in[:], 0.0)
+        nc.scalar.activation(out=warm_out[:], in_=warm_in[:], func=ACT.Exp)
+
+        bias_words = bias_in[:].bitcast(F32).rearrange("p w x -> p (w x)")
+        bias_all = keep.tile([P, 2 * HEADS, L * J], BF16)
+        bias_all_words = bias_all[:].rearrange("p a x -> p (a x)").bitcast(F32).rearrange(
+            "p (a l jp) -> p a l jp", a=2 * HEADS, jp=J // 2
+        )
+        for pair in range(HEADS):
+            spread = psum_t.tile([P, 2, J // 2, L], F32, tag="bank")
+            for a in range(2):
+                w, h = divmod(2 * pair + a, HEADS)
+                for jp in range(J // 2):
+                    word = w * (BIAS_SLOT // 2) + h * (J // 2) + jp
+                    nc.tensor.transpose(
+                        spread[:, a, jp, :],
+                        bias_words[:, word : word + 1].to_broadcast([P, P]),
+                        ident[:],
+                    )
+            nc.vector.tensor_copy(
+                out=bias_all_words[:, 2 * pair : 2 * pair + 2, :, :],
+                in_=spread[:].rearrange("p a jp l -> p a l jp"),
+            )
+
+        tok_grouped = keep.tile([P, L, PACK], BF16, align_bytes=64)
+        nc.vector.tensor_copy(out=tok_grouped[:], in_=tok_raw[:].rearrange("p t c -> p c t"))
+        tok_codes = keep.tile([P, L], U32, align_bytes=64)
+        tok_scales = keep.tile([P, L], U8, align_bytes=64)
+        nc.vector.quantize_mx(
+            out=tok_codes[:].bitcast(FP8X4),
+            scales=tok_scales[:],
+            in_=tok_grouped[:].rearrange("p c t -> p (c t)"),
+        )
+
+        grouped = {}
+        w_codes = {}
+        w_scales = {}
+        acc = {}
+        qk_bf = {}
+        qk_codes = {}
+        qk_scales = {}
+        score = psum_score.tile([P, HEADS, L], F32)
+
+        def transpose_weights(i):
+            words = w_raw[i][:].bitcast(F32)
+            grouped[i] = stage.tile([P, J * L * PACK], BF16, align_bytes=64, tag="grouped", name="grouped%d" % i)
+            grouped_words = grouped[i][:].bitcast(F32).rearrange("p (j l u) -> p j l u", j=J, u=HALVES)
+            for jp in range(J // 2):
+                flipped = psum_t.tile([P, 2, HALVES, L], F32, tag="bank")
+                for jj in range(2):
+                    for u in range(HALVES):
+                        first = ((2 * jp + jj) * HALVES + u) * P
+                        nc.tensor.transpose(flipped[:, jj, u, :], words[:, first : first + P], ident[:])
+                nc.scalar.copy(
+                    out=grouped_words[:, 2 * jp : 2 * jp + 2, :, :],
+                    in_=flipped[:].rearrange("p jj u l -> p jj l u"),
+                )
+
+        def quantise_weights(i):
+            w_codes[i] = keep.tile([P, J * L], U32, align_bytes=64, name="w_codes%d" % i)
+            w_scales[i] = keep.tile([P, J * L], U8, align_bytes=64, name="w_scales%d" % i)
+            nc.vector.quantize_mx(
+                out=w_codes[i][:].bitcast(FP8X4), scales=w_scales[i][:], in_=grouped[i][:]
+            )
+
+        def project(i):
+            acc[i] = psum_acc.tile([P, J * L], F32, tag="acc", name="acc%d" % i)
+            nc.tensor.matmul_mx(
+                out=acc[i][:],
+                lhsT=tok_codes[:].bitcast(FP8X4),
+                lhsT_scale=tok_scales[:],
+                rhs=w_codes[i][:].bitcast(FP8X4),
+                rhs_scale=w_scales[i][:],
+                start=True,
+                stop=True,
+            )
+
+        def add_bias(i):
+            w, h = chunks[i]
+            qk_bf[i] = keep.tile([P, L * J], BF16, align_bytes=64, name="qk_bf%d" % i)
+            nc.vector.tensor_tensor(
+                out=qk_bf[i][:].rearrange("p (l j) -> p l j", j=J),
+                in0=acc[i][:].rearrange("p (j l) -> p l j", j=J),
+                in1=bias_all[:, w * HEADS + h, :].rearrange("p (l j) -> p l j", j=J),
+                op=ALU.add,
+            )
+
+        def quantise_qk(i):
+            qk_codes[i] = keep.tile([P, L], U32, align_bytes=64, name="qk_codes%d" % i)
+            qk_scales[i] = keep.tile([P, L], U8, align_bytes=64, name="qk_scales%d" % i)
+            nc.vector.quantize_mx(
+                out=qk_codes[i][:].bitcast(FP8X4), scales=qk_scales[i][:], in_=qk_bf[i][:]
+            )
+
+        def multiply_qk(h):
+            q, k = 2 * h, 2 * h + 1
+            nc.tensor.matmul_mx(
+                out=score[:, h, :],
+                lhsT=qk_codes[q][:].bitcast(FP8X4),
+                lhsT_scale=qk_scales[q][:],
+                rhs=qk_codes[k][:].bitcast(FP8X4),
+                rhs_scale=qk_scales[k][:],
+                start=True,
+                stop=True,
+            )
+
+        def due(i):
+            return 0 <= i < n_chunks
+
+        for step in range(n_chunks + 5):
+            if due(step - 2):
+                project(step - 2)
+            if due(step - 4) and chunks[step - 4][0] == 1:
+                multiply_qk(chunks[step - 4][1])
+            if due(step):
+                transpose_weights(step)
+            if due(step - 1):
+                quantise_weights(step - 1)
+            if due(step - 2):
+                add_bias(step - 2)
+            if due(step - 3):
+                quantise_qk(step - 3)
+
+        top = keep.tile([P, L], F32)
+        nc.vector.tensor_reduce(
+            out=top[:], in_=score[:].rearrange("p h m -> p m h"), axis=mybir.AxisListType.X, op=ALU.max
+        )
+        shifted = keep.tile([P, HEADS, L], F32)
+        nc.vector.tensor_tensor(
+            out=shifted[:],
+            in0=score[:],
+            in1=top[:].unsqueeze(1).to_broadcast([P, HEADS, L]),
+            op=ALU.subtract,
+        )
+        expd = keep.tile([P, HEADS, L], F32)
+        nc.scalar.activation(out=expd[:], in_=shifted[:], func=ACT.Exp, scale=1.0 / math.sqrt(D))
+        total = keep.tile([P, L], F32)
+        nc.vector.tensor_reduce(
+            out=total[:], in_=expd[:].rearrange("p h m -> p m h"), axis=mybir.AxisListType.X, op=ALU.add
+        )
+        inverse = keep.tile([P, L], F32)
+        nc.vector.reciprocal(out=inverse[:], in_=total[:])
+        prob = keep.tile([P, HEADS, L], F32)
+        nc.vector.tensor_tensor(
+            out=prob[:],
+            in0=expd[:],
+            in1=inverse[:].unsqueeze(1).to_broadcast([P, HEADS, L]),
+            op=ALU.mult,
+        )
+        nc.sync.dma_start(out=out.rearrange("h l m -> l h m"), in_=prob[:])

@@ -21,6 +21,7 @@ J = D // L
 ROWS_PER_POSITION = HEADS * J
 HALVES = 2
 BIAS_SLOT = 16
+WARM_MATMULS = 5
 
 FLOPS = 2 * (2 * HEADS * D) * D * L + 2 * HEADS * L * L * D
 
@@ -66,6 +67,10 @@ def tile_selfattention_pa_s_kernel(tc, tokens, Wq, bq, Wk, bk, out):
         warm_out = keep.tile([P, 1], F32)
         nc.vector.memset(warm_in[:], 0.0)
         nc.scalar.activation(out=warm_out[:], in_=warm_in[:], func=ACT.Exp)
+
+        unread = psum_acc.tile([P, P], F32, tag="acc")
+        for n in range(WARM_MATMULS):
+            nc.tensor.matmul(out=unread[:], lhsT=ident[:], rhs=ident[:], start=True, stop=True)
 
         bias_words = bias_in[:].bitcast(F32).rearrange("p w x -> p (w x)")
         bias_all = keep.tile([P, 2 * HEADS, L * J], BF16)

@@ -20,6 +20,8 @@ L = 128
 J = D // L
 ROWS_PER_POSITION = HEADS * J
 HALVES = 2
+PIECES = 2
+ROWS_PER_PIECE = J // PIECES
 BIAS_SLOT = 16
 WARM_MATMULS = 5
 
@@ -35,7 +37,7 @@ def tile_selfattention_pa_s_kernel(tc, tokens, Wq, bq, Wk, bk, out):
 
     with ExitStack() as ctx:
         keep = ctx.enter_context(tc.tile_pool(name="keep", bufs=1))
-        stage = ctx.enter_context(tc.tile_pool(name="stage", bufs=3))
+        stage = ctx.enter_context(tc.tile_pool(name="stage", bufs=4))
         psum_t = ctx.enter_context(tc.psum_pool(name="psum_t", bufs=4))
         psum_acc = ctx.enter_context(tc.psum_pool(name="psum_acc", bufs=3))
         psum_score = ctx.enter_context(tc.psum_pool(name="psum_score", bufs=1))
@@ -53,13 +55,16 @@ def tile_selfattention_pa_s_kernel(tc, tokens, Wq, bq, Wk, bk, out):
             in_=tokens.rearrange("(u p e) c -> p u (e c)", u=HALVES, e=2),
         )
         w_raw = []
-        for i, (w, h) in enumerate(chunks):
-            raw = keep.tile([P, J * D], BF16, name="w_raw%d" % i)
-            nc.sync.dma_start(
-                out=raw[:],
-                in_=weights[w].rearrange("(l h j) k -> l h (j k)", h=HEADS, j=J)[:, h, :],
-            )
-            w_raw.append(raw)
+        for w, h in chunks:
+            for jp in range(PIECES):
+                raw = keep.tile([P, ROWS_PER_PIECE * D], BF16, name="w_raw%d" % len(w_raw))
+                nc.sync.dma_start(
+                    out=raw[:],
+                    in_=weights[w].rearrange(
+                        "(l h jp jj) k -> l h jp (jj k)", h=HEADS, jp=PIECES, jj=ROWS_PER_PIECE
+                    )[:, h, jp, :],
+                )
+                w_raw.append(raw)
 
         ident = keep.tile([P, P], F32)
         make_identity(nc, ident[:])
@@ -112,26 +117,29 @@ def tile_selfattention_pa_s_kernel(tc, tokens, Wq, bq, Wk, bk, out):
         qk_scales = {}
         score = psum_score.tile([P, HEADS, L], F32)
 
-        def transpose_weights(i):
-            words = w_raw[i][:].bitcast(F32)
-            grouped[i] = stage.tile([P, J * L * PACK], BF16, align_bytes=64, tag="grouped", name="grouped%d" % i)
-            grouped_words = grouped[i][:].bitcast(F32).rearrange("p (j l u) -> p j l u", j=J, u=HALVES)
-            for jp in range(J // 2):
-                flipped = psum_t.tile([P, 2, HALVES, L], F32, tag="bank")
-                for jj in range(2):
-                    for u in range(HALVES):
-                        first = ((2 * jp + jj) * HALVES + u) * P
-                        nc.tensor.transpose(flipped[:, jj, u, :], words[:, first : first + P], ident[:])
-                nc.scalar.copy(
-                    out=grouped_words[:, 2 * jp : 2 * jp + 2, :, :],
-                    in_=flipped[:].rearrange("p jj u l -> p jj l u"),
-                )
+        def transpose_weights(t):
+            words = w_raw[t][:].bitcast(F32)
+            flipped = psum_t.tile([P, ROWS_PER_PIECE, HALVES, L], F32, tag="bank")
+            for jj in range(ROWS_PER_PIECE):
+                for u in range(HALVES):
+                    first = (jj * HALVES + u) * P
+                    nc.tensor.transpose(flipped[:, jj, u, :], words[:, first : first + P], ident[:])
+            grouped[t] = stage.tile(
+                [P, ROWS_PER_PIECE * L * PACK], BF16, align_bytes=64, tag="grouped", name="grouped%d" % t
+            )
+            nc.scalar.copy(
+                out=grouped[t][:].bitcast(F32).rearrange("p (jj l u) -> p jj l u", jj=ROWS_PER_PIECE, u=HALVES),
+                in_=flipped[:].rearrange("p jj u l -> p jj l u"),
+            )
 
-        def quantise_weights(i):
-            w_codes[i] = keep.tile([P, J * L], U32, align_bytes=64, name="w_codes%d" % i)
-            w_scales[i] = keep.tile([P, J * L], U8, align_bytes=64, name="w_scales%d" % i)
+        def quantise_weights(t):
+            i, jp = divmod(t, PIECES)
+            if jp == 0:
+                w_codes[i] = keep.tile([P, J * L], U32, align_bytes=64, name="w_codes%d" % i)
+                w_scales[i] = keep.tile([P, J * L], U8, align_bytes=64, name="w_scales%d" % i)
+            cols = slice(jp * ROWS_PER_PIECE * L, (jp + 1) * ROWS_PER_PIECE * L)
             nc.vector.quantize_mx(
-                out=w_codes[i][:].bitcast(FP8X4), scales=w_scales[i][:], in_=grouped[i][:]
+                out=w_codes[i][:, cols].bitcast(FP8X4), scales=w_scales[i][:, cols], in_=grouped[t][:]
             )
 
         def project(i):
@@ -179,18 +187,18 @@ def tile_selfattention_pa_s_kernel(tc, tokens, Wq, bq, Wk, bk, out):
             return 0 <= i < n_chunks
 
         for step in range(n_chunks + 5):
+            for jp in range(PIECES):
+                if due(step):
+                    transpose_weights(PIECES * step + jp)
+                if due(step - 1):
+                    quantise_weights(PIECES * (step - 1) + jp)
             if due(step - 2):
                 project(step - 2)
-            if due(step - 4) and chunks[step - 4][0] == 1:
-                multiply_qk(chunks[step - 4][1])
-            if due(step):
-                transpose_weights(step)
-            if due(step - 1):
-                quantise_weights(step - 1)
-            if due(step - 2):
                 add_bias(step - 2)
             if due(step - 3):
                 quantise_qk(step - 3)
+            if due(step - 4) and chunks[step - 4][0] == 1:
+                multiply_qk(chunks[step - 4][1])
 
         top = keep.tile([P, L], F32)
         nc.vector.tensor_reduce(

@@ -41,7 +41,6 @@ def tile_selfattention_pa_s_kernel(tc, tokens, Wq, bq, Wk, bk, out):
         psum_t = ctx.enter_context(tc.psum_pool(name="psum_t", bufs=4))
         psum_acc = ctx.enter_context(tc.psum_pool(name="psum_acc", bufs=3))
         psum_score = ctx.enter_context(tc.psum_pool(name="psum_score", bufs=1))
-        ctx.enter_context(tc.manual_schedule())
 
         bias_in = keep.tile([P, 2, BIAS_SLOT], BF16)
         for w in range(2):

from contextlib import ExitStack
import math

import concourse.mybir as mybir
from concourse.masks import make_identity

BF16 = mybir.dt.bfloat16
F32 = mybir.dt.float32
U32 = mybir.dt.uint32
U8 = mybir.dt.uint8
FP8X4 = mybir.dt.float8_e4m3fn_x4
ALU = mybir.AluOpType
ACT = mybir.ActivationFunctionType

P = 128
PACK = 4
HEADS = 3
D = 512
L = 128
J = D // L
ROWS_PER_POSITION = HEADS * J
HALVES = 2
PIECES = 2
ROWS_PER_PIECE = J // PIECES
BIAS_SLOT = 16
WARM_MATMULS = 5

FLOPS = 2 * (2 * HEADS * D) * D * L + 2 * HEADS * L * L * D


def tile_selfattention_pa_s_kernel(tc, tokens, Wq, bq, Wk, bk, out):
    nc = tc.nc
    weights = (Wq, Wk)
    biases = (bq, bk)
    chunks = [(w, h) for h in range(HEADS) for w in range(2)]
    n_chunks = len(chunks)

    with ExitStack() as ctx:
        keep = ctx.enter_context(tc.tile_pool(name="keep", bufs=1))
        stage = ctx.enter_context(tc.tile_pool(name="stage", bufs=4))
        psum_t = ctx.enter_context(tc.psum_pool(name="psum_t", bufs=4))
        psum_acc = ctx.enter_context(tc.psum_pool(name="psum_acc", bufs=3))
        psum_score = ctx.enter_context(tc.psum_pool(name="psum_score", bufs=1))

        bias_in = keep.tile([P, 2, BIAS_SLOT], BF16)
        for w in range(2):
            nc.scalar.dma_start(
                out=bias_in[:, w, 0:ROWS_PER_POSITION],
                in_=biases[w].rearrange("(l r) -> l r", r=ROWS_PER_POSITION),
            )
        tok_raw = keep.tile([P, PACK, L], BF16)
        nc.scalar.dma_start(
            out=tok_raw[:].rearrange("p (u e) c -> p u (e c)", u=HALVES),
            in_=tokens.rearrange("(u p e) c -> p u (e c)", u=HALVES, e=2),
        )
        w_raw = []
        for w, h in chunks:
            for jp in range(PIECES):
                raw = keep.tile([P, ROWS_PER_PIECE * D], BF16, name="w_raw%d" % len(w_raw))
                nc.sync.dma_start(
                    out=raw[:],
                    in_=weights[w].rearrange(
                        "(l h jp jj) k -> l h jp (jj k)", h=HEADS, jp=PIECES, jj=ROWS_PER_PIECE
                    )[:, h, jp, :],
                )
                w_raw.append(raw)

        ident = keep.tile([P, P], F32)
        make_identity(nc, ident[:])
        warm_in = keep.tile([P, 1], F32)
        warm_out = keep.tile([P, 1], F32)
        nc.vector.memset(warm_in[:], 0.0)
        nc.scalar.activation(out=warm_out[:], in_=warm_in[:], func=ACT.Exp)

        unread = psum_acc.tile([P, P], F32, tag="acc")
        for n in range(WARM_MATMULS):
            nc.tensor.matmul(out=unread[:], lhsT=ident[:], rhs=ident[:], start=True, stop=True)

        bias_words = bias_in[:].bitcast(F32).rearrange("p w x -> p (w x)")
        bias_all = keep.tile([P, 2 * HEADS, L * J], BF16)
        bias_all_words = bias_all[:].rearrange("p a x -> p (a x)").bitcast(F32).rearrange(
            "p (a l jp) -> p a l jp", a=2 * HEADS, jp=J // 2
        )
        for pair in range(HEADS):
            spread = psum_t.tile([P, 2, J // 2, L], F32, tag="bank")
            for a in range(2):
                w, h = divmod(2 * pair + a, HEADS)
                for jp in range(J // 2):
                    word = w * (BIAS_SLOT // 2) + h * (J // 2) + jp
                    nc.tensor.transpose(
                        spread[:, a, jp, :],
                        bias_words[:, word : word + 1].to_broadcast([P, P]),
                        ident[:],
                    )
            nc.vector.tensor_copy(
                out=bias_all_words[:, 2 * pair : 2 * pair + 2, :, :],
                in_=spread[:].rearrange("p a jp l -> p a l jp"),
            )

        tok_grouped = keep.tile([P, L, PACK], BF16, align_bytes=64)
        nc.vector.tensor_copy(out=tok_grouped[:], in_=tok_raw[:].rearrange("p t c -> p c t"))
        tok_codes = keep.tile([P, L], U32, align_bytes=64)
        tok_scales = keep.tile([P, L], U8, align_bytes=64)
        nc.vector.quantize_mx(
            out=tok_codes[:].bitcast(FP8X4),
            scales=tok_scales[:],
            in_=tok_grouped[:].rearrange("p c t -> p (c t)"),
        )

        grouped = {}
        w_codes = {}
        w_scales = {}
        acc = {}
        qk_bf = {}
        qk_codes = {}
        qk_scales = {}
        score = psum_score.tile([P, HEADS, L], F32)

        def transpose_weights(t):
            words = w_raw[t][:].bitcast(F32)
            flipped = psum_t.tile([P, ROWS_PER_PIECE, HALVES, L], F32, tag="bank")
            for jj in range(ROWS_PER_PIECE):
                for u in range(HALVES):
                    first = (jj * HALVES + u) * P
                    nc.tensor.transpose(flipped[:, jj, u, :], words[:, first : first + P], ident[:])
            grouped[t] = stage.tile(
                [P, ROWS_PER_PIECE * L * PACK], BF16, align_bytes=64, tag="grouped", name="grouped%d" % t
            )
            nc.scalar.copy(
                out=grouped[t][:].bitcast(F32).rearrange("p (jj l u) -> p jj l u", jj=ROWS_PER_PIECE, u=HALVES),
                in_=flipped[:].rearrange("p jj u l -> p jj l u"),
            )

        def quantise_weights(t):
            i, jp = divmod(t, PIECES)
            if jp == 0:
                w_codes[i] = keep.tile([P, J * L], U32, align_bytes=64, name="w_codes%d" % i)
                w_scales[i] = keep.tile([P, J * L], U8, align_bytes=64, name="w_scales%d" % i)
            cols = slice(jp * ROWS_PER_PIECE * L, (jp + 1) * ROWS_PER_PIECE * L)
            nc.vector.quantize_mx(
                out=w_codes[i][:, cols].bitcast(FP8X4), scales=w_scales[i][:, cols], in_=grouped[t][:]
            )

        def project(i):
            acc[i] = psum_acc.tile([P, J * L], F32, tag="acc", name="acc%d" % i)
            nc.tensor.matmul_mx(
                out=acc[i][:],
                lhsT=tok_codes[:].bitcast(FP8X4),
                lhsT_scale=tok_scales[:],
                rhs=w_codes[i][:].bitcast(FP8X4),
                rhs_scale=w_scales[i][:],
                start=True,
                stop=True,
            )

        def add_bias(i):
            w, h = chunks[i]
            qk_bf[i] = keep.tile([P, L * J], BF16, align_bytes=64, name="qk_bf%d" % i)
            nc.vector.tensor_tensor(
                out=qk_bf[i][:].rearrange("p (l j) -> p l j", j=J),
                in0=acc[i][:].rearrange("p (j l) -> p l j", j=J),
                in1=bias_all[:, w * HEADS + h, :].rearrange("p (l j) -> p l j", j=J),
                op=ALU.add,
            )

        def quantise_qk(i):
            qk_codes[i] = keep.tile([P, L], U32, align_bytes=64, name="qk_codes%d" % i)
            qk_scales[i] = keep.tile([P, L], U8, align_bytes=64, name="qk_scales%d" % i)
            nc.vector.quantize_mx(
                out=qk_codes[i][:].bitcast(FP8X4), scales=qk_scales[i][:], in_=qk_bf[i][:]
            )

        def multiply_qk(h):
            q, k = 2 * h, 2 * h + 1
            nc.tensor.matmul_mx(
                out=score[:, h, :],
                lhsT=qk_codes[q][:].bitcast(FP8X4),
                lhsT_scale=qk_scales[q][:],
                rhs=qk_codes[k][:].bitcast(FP8X4),
                rhs_scale=qk_scales[k][:],
                start=True,
                stop=True,
            )

        def due(i):
            return 0 <= i < n_chunks

        for step in range(n_chunks + 5):
            for jp in range(PIECES):
                if due(step):
                    transpose_weights(PIECES * step + jp)
                if due(step - 1):
                    quantise_weights(PIECES * (step - 1) + jp)
            if due(step - 2):
                project(step - 2)
                add_bias(step - 2)
            if due(step - 3):
                quantise_qk(step - 3)
            if due(step - 4) and chunks[step - 4][0] == 1:
                multiply_qk(chunks[step - 4][1])

        top = keep.tile([P, L], F32)
        nc.vector.tensor_reduce(
            out=top[:], in_=score[:].rearrange("p h m -> p m h"), axis=mybir.AxisListType.X, op=ALU.max
        )
        shifted = keep.tile([P, HEADS, L], F32)
        nc.vector.tensor_tensor(
            out=shifted[:],
            in0=score[:],
            in1=top[:].unsqueeze(1).to_broadcast([P, HEADS, L]),
            op=ALU.subtract,
        )
        expd = keep.tile([P, HEADS, L], F32)
        nc.scalar.activation(out=expd[:], in_=shifted[:], func=ACT.Exp, scale=1.0 / math.sqrt(D))
        total = keep.tile([P, L], F32)
        nc.vector.tensor_reduce(
            out=total[:], in_=expd[:].rearrange("p h m -> p m h"), axis=mybir.AxisListType.X, op=ALU.add
        )
        inverse = keep.tile([P, L], F32)
        nc.vector.reciprocal(out=inverse[:], in_=total[:])
        prob = keep.tile([P, HEADS, L], F32)
        nc.vector.tensor_tensor(
            out=prob[:],
            in0=expd[:],
            in1=inverse[:].unsqueeze(1).to_broadcast([P, HEADS, L]),
            op=ALU.mult,
        )
        nc.sync.dma_start(out=out.rearrange("h l m -> l h m"), in_=prob[:])
